import numpy as np
import ml_dtypes


def mxq(x, axis, fmt="e4m3"):
    dtype, down = {"e4m3": (ml_dtypes.float8_e4m3fn, 7), "e5m2": (ml_dtypes.float8_e5m2, 14)}[fmt]
    v = np.moveaxis(np.asarray(x, np.float32).astype(ml_dtypes.bfloat16).astype(np.float64), axis, -1)
    blocks = v.reshape(v.shape[:-1] + (-1, 32))
    amax = np.abs(blocks).max(-1, keepdims=True)
    byte = np.maximum(np.where(amax > 0, np.frexp(amax)[1] - 1 + 127, 0) - down, 1)
    scale = np.exp2(byte - 127.0)
    codes = (blocks / scale).astype(np.float32).astype(dtype).astype(np.float64)
    return np.moveaxis((codes * scale).reshape(v.shape), -1, axis)


WIDE = False


def mx_kscale(k):
    if not WIDE:
        return np.ones(k)
    levels = np.array([10, -10, 5, -5, 0])
    a = np.random.permutation(np.resize(levels, k // 512 * 4)).reshape(k // 512, 4)
    idx = np.arange(k)
    return np.exp2(a[idx // 512, idx % 128 // 32])


BF16 = ml_dtypes.bfloat16


def bf(x):
    return np.asarray(x, np.float32).astype(BF16)


def f64(x):
    return np.asarray(x).astype(np.float64)


B, C, CK, H, W = 32, 512, 512, 16, 16
N = H * W


def setup_inputs():
    s, t = mx_kscale(C), mx_kscale(CK)
    return {
        "x": bf(np.random.standard_normal((B, C, H, W)) * s[None, :, None, None]),
        "Wq": bf(np.random.standard_normal((CK, C)) / np.sqrt(C) / s[None, :] * t[:, None]),
        "bq": bf(np.random.standard_normal(CK) * 0.3 * t),
        "Wk": bf(np.random.standard_normal((CK, C)) / np.sqrt(C) / s[None, :] / t[:, None]),
        "bk": bf(np.random.standard_normal(CK) * 0.3 / t),
        "fg_sim": bf(np.random.uniform(size=(B, N, N))),
    }


def reference(x, Wq, bq, Wk, bk, fg_sim):
    xq = mxq(f64(x).reshape(B, C, N), 1, "e4m3")
    query = (mxq(f64(Wq), 1, "e4m3") @ xq).transpose(0, 2, 1) + f64(bq)
    key = (mxq(f64(Wk), 1, "e4m3") @ xq) + f64(bk)[None, :, None]
    sim = (mxq(query, 2, "e4m3") @ mxq(key, 1, "e4m3")) * CK ** -0.5
    return sim * f64(fg_sim)

@@ -1,0 +1,208 @@
+from contextlib import ExitStack
+
+import concourse.mybir as mybir
+from concourse.masks import make_identity
+
+F32 = mybir.dt.float32
+BF16 = mybir.dt.bfloat16
+U32 = mybir.dt.uint32
+U8 = mybir.dt.uint8
+FP8X4 = mybir.dt.float8_e4m3fn_x4
+IDENTITY = mybir.ActivationFunctionType.Identity
+MULT = mybir.AluOpType.mult
+
+IMAGES = 32
+C = 512
+CK = 512
+N = 256
+P = 128
+PACK = 4
+PAIR = 2
+COLS = PAIR * N
+ROUNDS = IMAGES // PAIR
+ROW_TILES = N // P
+RUN = 4
+AHEAD = 2
+
+FLOPS = IMAGES * (2 * 2 * CK * C * N + 2 * N * N * CK)
+
+
+def regroup(copy, grouped, planes):
+    copy(
+        out=grouped.rearrange("p (c i) t -> p c t i", i=RUN),
+        in_=planes.rearrange("p t (c i) -> p c t i", i=RUN),
+    )
+
+
+def tile_sgan_pa_t_kernel(tc, x, Wq, bq, Wk, bk, fg_sim, out):
+    nc = tc.nc
+    with ExitStack() as ctx:
+        consts = ctx.enter_context(tc.tile_pool(name="consts", bufs=1))
+        inputs = ctx.enter_context(tc.tile_pool(name="inputs", bufs=ROUNDS))
+        x_pool = ctx.enter_context(tc.tile_pool(name="x_pool", bufs=AHEAD + 2))
+        work = ctx.enter_context(tc.tile_pool(name="work", bufs=2))
+        results = ctx.enter_context(tc.tile_pool(name="results", bufs=8))
+        banks = ctx.enter_context(tc.psum_pool(name="banks", bufs=6))
+        sims = ctx.enter_context(tc.psum_pool(name="sims", bufs=2))
+
+        x_raw = {}
+        fg = {}
+
+        def load_x(k):
+            raw = inputs.tile([P, PAIR, PACK, N], BF16, name="x_raw")
+            nc.sync.dma_start(
+                out=raw[:].rearrange("p b t n -> p b (t n)"),
+                in_=x[PAIR * k : PAIR * (k + 1)].rearrange("b (p t) h w -> p b (t h w)", t=PACK),
+            )
+            x_raw[k] = raw
+
+        def load_fg(k):
+            mask = inputs.tile([P, PAIR, ROW_TILES, N], BF16, name="fg")
+            nc.sync.dma_start(
+                out=mask[:],
+                in_=fg_sim[PAIR * k : PAIR * (k + 1)].rearrange("b (i p) m -> p b i m", p=P),
+            )
+            fg[k] = mask
+
+        load_x(0)
+        w_raw = {}
+        bias_bf16 = {}
+        for w, weight, b_vec in (("q", Wq, bq), ("k", Wk, bk)):
+            raw = consts.tile([P, PACK, C], BF16, name="w_raw_" + w)
+            nc.sync.dma_start(out=raw[:], in_=weight.rearrange("(p t) c -> p t c", t=PACK))
+            w_raw[w] = raw
+            b_raw = consts.tile([P, PACK], BF16, name="bias_bf16_" + w)
+            nc.scalar.dma_start(out=b_raw[:], in_=b_vec.rearrange("(p t) -> p t", t=PACK))
+            bias_bf16[w] = b_raw
+        for k in range(1, ROUNDS):
+            load_x(k)
+            load_fg(k - 1)
+        load_fg(ROUNDS - 1)
+
+        ident = consts.tile([P, P], F32, name="ident")
+        make_identity(nc, ident[:])
+
+        w_codes = {}
+        w_scales = {}
+        bias = {}
+        for w in ("q", "k"):
+            b_f32 = consts.tile([P, PACK], F32, name="bias_" + w)
+            nc.vector.tensor_copy(out=b_f32[:], in_=bias_bf16[w][:])
+            bias[w] = b_f32
+
+            words = w_raw[w][:].bitcast(F32).rearrange("j t (q u) -> j t u q", u=2)
+            grouped = consts.tile([P, PACK, P, PACK], BF16, align_bytes=64, name="w_grouped_" + w)
+            grouped_words = grouped[:].bitcast(F32)
+            for half in range(2):
+                flipped = banks.tile([P, 2, 2, P], F32, tag="bank", name="flipped")
+                for t in range(2):
+                    for u in range(2):
+                        nc.tensor.transpose(flipped[:, t, u, :], words[:, 2 * half + t, u, :], ident[:])
+                copy = nc.vector.tensor_copy if half == 0 else nc.scalar.copy
+                copy(
+                    out=grouped_words[:, 2 * half : 2 * half + 2, :, :],
+                    in_=flipped[:].rearrange("q t u j -> q t j u"),
+                )
+            codes = consts.tile([P, PACK * P], U32, align_bytes=64, name="w_codes_" + w)
+            scales = consts.tile([P, PACK * P], U8, align_bytes=64, name="w_scales_" + w)
+            nc.vector.quantize_mx(
+                out=codes[:].bitcast(FP8X4),
+                scales=scales[:],
+                in_=grouped[:].rearrange("q t j c -> q (t j c)"),
+            )
+            w_codes[w] = codes
+            w_scales[w] = scales
+
+        x_mx = {}
+        planes = {}
+        qk_mx = {}
+
+        def quantise_x(k):
+            grouped = x_pool.tile([P, PAIR, N, PACK], BF16, align_bytes=64, name="x_grouped")
+            regroup(nc.vector.tensor_copy, grouped[:, 0], x_raw[k][:, 0])
+            regroup(nc.scalar.copy, grouped[:, 1], x_raw[k][:, 1])
+            codes = x_pool.tile([P, COLS], U32, align_bytes=64, name="x_codes")
+            scales = x_pool.tile([P, COLS], U8, align_bytes=64, name="x_scales")
+            nc.vector.quantize_mx(
+                out=codes[:].bitcast(FP8X4),
+                scales=scales[:],
+                in_=grouped[:].rearrange("p b n t -> p (b n t)"),
+            )
+            x_mx[k] = (codes, scales)
+
+        def project(k):
+            codes, scales = x_mx[k]
+            for w in ("q", "k"):
+                plane = work.tile([P, PACK, COLS], BF16, name="planes_" + w)
+                for t in range(PACK):
+                    bank = banks.tile([P, COLS], F32, tag="bank", name="bank")
+                    nc.tensor.matmul_mx(
+                        out=bank[:],
+                        lhsT=w_codes[w][:, t * P : (t + 1) * P].bitcast(FP8X4),
+                        lhsT_scale=w_scales[w][:, t * P : (t + 1) * P],
+                        rhs=codes[:].bitcast(FP8X4),
+                        rhs_scale=scales[:],
+                        start=True,
+                        stop=True,
+                    )
+                    nc.scalar.activation(
+                        out=plane[:, t, :], in_=bank[:], func=IDENTITY, bias=bias[w][:, t : t + 1], scale=1.0
+                    )
+                planes[(k, w)] = plane
+
+        def requantise(k):
+            grouped = {}
+            for w in ("q", "k"):
+                g = work.tile([P, COLS, PACK], BF16, align_bytes=64, name="grouped_" + w)
+                regroup(nc.vector.tensor_copy, g[:], planes[(k, w)][:])
+                grouped[w] = g
+            for w in ("q", "k"):
+                codes = work.tile([P, COLS], U32, align_bytes=64, name="codes_" + w)
+                scales = work.tile([P, COLS], U8, align_bytes=64, name="scales_" + w)
+                nc.vector.quantize_mx(
+                    out=codes[:].bitcast(FP8X4),
+                    scales=scales[:],
+                    in_=grouped[w][:].rearrange("p n t -> p (n t)"),
+                )
+                qk_mx[(k, w)] = (codes, scales)
+
+        def similarity(k):
+            q_codes, q_scales = qk_mx[(k, "q")]
+            k_codes, k_scales = qk_mx[(k, "k")]
+            for b in range(PAIR):
+                sim = sims.tile([P, ROW_TILES, N], F32, name="sim")
+                for i in range(ROW_TILES):
+                    rows = slice(b * N + i * P, b * N + (i + 1) * P)
+                    nc.tensor.matmul_mx(
+                        out=sim[:, i, :],
+                        lhsT=q_codes[:, rows].bitcast(FP8X4),
+                        lhsT_scale=q_scales[:, rows],
+                        rhs=k_codes[:, b * N : (b + 1) * N].bitcast(FP8X4),
+                        rhs_scale=k_scales[:, b * N : (b + 1) * N],
+                        start=True,
+                        stop=True,
+                    )
+                result = results.tile([P, ROW_TILES, N], F32, name="result")
+                nc.vector.scalar_tensor_tensor(
+                    out=result[:].rearrange("p i m -> p (i m)"),
+                    in0=sim[:].rearrange("p i m -> p (i m)"),
+                    scalar=CK**-0.5,
+                    in1=fg[k][:, b].rearrange("p i m -> p (i m)"),
+                    op0=MULT,
+                    op1=MULT,
+                )
+                nc.sync.dma_start(
+                    out=out[PAIR * k + b].rearrange("(i p) m -> p i m", p=P), in_=result[:]
+                )
+
+        for k in range(AHEAD):
+            quantise_x(k)
+        for k in range(ROUNDS + 2):
+            if k + AHEAD < ROUNDS:
+                quantise_x(k + AHEAD)
+            if k < ROUNDS:
+                project(k)
+            if 1 <= k <= ROUNDS:
+                requantise(k - 1)
+            if k >= 2:
+                similarity(k - 2)

@@ -10,6 +10,7 @@ U8 = mybir.dt.uint8
 FP8X4 = mybir.dt.float8_e4m3fn_x4
 IDENTITY = mybir.ActivationFunctionType.Identity
 MULT = mybir.AluOpType.mult
+ADD = mybir.AluOpType.add
 
 IMAGES = 32
 C = 512
@@ -119,7 +120,14 @@ def tile_sgan_pa_t_kernel(tc, x, Wq, bq, Wk, bk, fg_sim, out):
 
         def quantise_x(k):
             grouped = x_pool.tile([P, PAIR, N, PACK], BF16, align_bytes=64, name="x_grouped")
-            regroup(nc.vector.tensor_copy, grouped[:, 0], x_raw[k][:, 0])
+            nc.gpsimd.tensor_scalar(
+                out=grouped[:, 0],
+                in0=x_raw[k][:, 0].rearrange("p t n -> p n t"),
+                scalar1=1.0,
+                scalar2=0.0,
+                op0=MULT,
+                op1=ADD,
+            )
             regroup(nc.scalar.copy, grouped[:, 1], x_raw[k][:, 1])
             codes = x_pool.tile([P, COLS], U32, align_bytes=64, name="x_codes")
             scales = x_pool.tile([P, COLS], U8, align_bytes=64, name="x_scales")

@@ -10,7 +10,6 @@ U8 = mybir.dt.uint8
 FP8X4 = mybir.dt.float8_e4m3fn_x4
 IDENTITY = mybir.ActivationFunctionType.Identity
 MULT = mybir.AluOpType.mult
-ADD = mybir.AluOpType.add
 
 IMAGES = 32
 C = 512
@@ -19,13 +18,16 @@ N = 256
 P = 128
 PACK = 4
 PAIR = 2
-COLS = PAIR * N
-ROUNDS = IMAGES // PAIR
 ROW_TILES = N // P
 RUN = 4
 AHEAD = 2
+ROUND_IMAGES = (1, 1) + (2,) * 14 + (1, 1)
+ROUNDS = len(ROUND_IMAGES)
+PROJECTIONS = ("q", "k")
 
 FLOPS = IMAGES * (2 * 2 * CK * C * N + 2 * N * N * CK)
+
+assert sum(ROUND_IMAGES) == IMAGES
 
 
 def regroup(copy, grouped, planes):
@@ -39,46 +41,49 @@ def tile_sgan_pa_t_kernel(tc, x, Wq, bq, Wk, bk, fg_sim, out):
     nc = tc.nc
     with ExitStack() as ctx:
         consts = ctx.enter_context(tc.tile_pool(name="consts", bufs=1))
-        inputs = ctx.enter_context(tc.tile_pool(name="inputs", bufs=ROUNDS))
+        inputs = ctx.enter_context(tc.tile_pool(name="inputs", bufs=IMAGES))
         x_pool = ctx.enter_context(tc.tile_pool(name="x_pool", bufs=AHEAD + 2))
         work = ctx.enter_context(tc.tile_pool(name="work", bufs=2))
-        results = ctx.enter_context(tc.tile_pool(name="results", bufs=8))
+        results = ctx.enter_context(tc.tile_pool(name="results", bufs=12))
         banks = ctx.enter_context(tc.psum_pool(name="banks", bufs=6))
         sims = ctx.enter_context(tc.psum_pool(name="sims", bufs=2))
 
+        def images_of(k):
+            first = sum(ROUND_IMAGES[:k])
+            return range(first, first + ROUND_IMAGES[k])
+
         x_raw = {}
         fg = {}
-
-        def load_x(k):
-            raw = inputs.tile([P, PAIR, PACK, N], BF16, name="x_raw")
-            nc.sync.dma_start(
-                out=raw[:].rearrange("p b t n -> p b (t n)"),
-                in_=x[PAIR * k : PAIR * (k + 1)].rearrange("b (p t) h w -> p b (t h w)", t=PACK),
-            )
-            x_raw[k] = raw
-
-        def load_fg(k):
-            mask = inputs.tile([P, PAIR, ROW_TILES, N], BF16, name="fg")
-            nc.sync.dma_start(
-                out=mask[:],
-                in_=fg_sim[PAIR * k : PAIR * (k + 1)].rearrange("b (i p) m -> p b i m", p=P),
-            )
-            fg[k] = mask
-
-        load_x(0)
         w_raw = {}
         bias_bf16 = {}
-        for w, weight, b_vec in (("q", Wq, bq), ("k", Wk, bk)):
+
+        def load_x(image):
+            raw = inputs.tile([P, PACK, N], BF16, name="x_raw")
+            nc.sync.dma_start(out=raw[:], in_=x[image].rearrange("(p t) h w -> p t (h w)", t=PACK))
+            x_raw[image] = raw
+
+        def load_fg(image):
+            mask = inputs.tile([P, ROW_TILES, N], BF16, name="fg")
+            nc.sync.dma_start(out=mask[:], in_=fg_sim[image].rearrange("(i p) m -> p i m", p=P))
+            fg[image] = mask
+
+        def load_weight(w, weight, b_vec):
             raw = consts.tile([P, PACK, C], BF16, name="w_raw_" + w)
             nc.sync.dma_start(out=raw[:], in_=weight.rearrange("(p t) c -> p t c", t=PACK))
             w_raw[w] = raw
             b_raw = consts.tile([P, PACK], BF16, name="bias_bf16_" + w)
             nc.scalar.dma_start(out=b_raw[:], in_=b_vec.rearrange("(p t) -> p t", t=PACK))
             bias_bf16[w] = b_raw
-        for k in range(1, ROUNDS):
-            load_x(k)
-            load_fg(k - 1)
-        load_fg(ROUNDS - 1)
+
+        load_x(0)
+        load_weight("q", Wq, bq)
+        load_x(1)
+        load_weight("k", Wk, bk)
+        for image in range(2, IMAGES):
+            load_x(image)
+            load_fg(image - 2)
+        load_fg(IMAGES - 2)
+        load_fg(IMAGES - 1)
 
         ident = consts.tile([P, P], F32, name="ident")
         make_identity(nc, ident[:])
@@ -86,7 +91,7 @@ def tile_sgan_pa_t_kernel(tc, x, Wq, bq, Wk, bk, fg_sim, out):
         w_codes = {}
         w_scales = {}
         bias = {}
-        for w in ("q", "k"):
+        for w in PROJECTIONS:
             b_f32 = consts.tile([P, PACK], F32, name="bias_" + w)
             nc.vector.tensor_copy(out=b_f32[:], in_=bias_bf16[w][:])
             bias[w] = b_f32
@@ -94,23 +99,19 @@ def tile_sgan_pa_t_kernel(tc, x, Wq, bq, Wk, bk, fg_sim, out):
             words = w_raw[w][:].bitcast(F32).rearrange("j t (q u) -> j t u q", u=2)
             grouped = consts.tile([P, PACK, P, PACK], BF16, align_bytes=64, name="w_grouped_" + w)
             grouped_words = grouped[:].bitcast(F32)
-            for half in range(2):
-                flipped = banks.tile([P, 2, 2, P], F32, tag="bank", name="flipped")
-                for t in range(2):
-                    for u in range(2):
-                        nc.tensor.transpose(flipped[:, t, u, :], words[:, 2 * half + t, u, :], ident[:])
-                copy = nc.vector.tensor_copy if half == 0 else nc.scalar.copy
-                copy(
-                    out=grouped_words[:, 2 * half : 2 * half + 2, :, :],
-                    in_=flipped[:].rearrange("q t u j -> q t j u"),
-                )
             codes = consts.tile([P, PACK * P], U32, align_bytes=64, name="w_codes_" + w)
             scales = consts.tile([P, PACK * P], U8, align_bytes=64, name="w_scales_" + w)
-            nc.vector.quantize_mx(
-                out=codes[:].bitcast(FP8X4),
-                scales=scales[:],
-                in_=grouped[:].rearrange("q t j c -> q (t j c)"),
-            )
+            for t in range(PACK):
+                flipped = banks.tile([P, 2, P], F32, tag="bank", name="flipped")
+                for u in range(2):
+                    nc.tensor.transpose(flipped[:, u, :], words[:, t, u, :], ident[:])
+                copy = nc.vector.tensor_copy if t % 2 == 0 else nc.scalar.copy
+                copy(out=grouped_words[:, t], in_=flipped[:].rearrange("q u j -> q j u"))
+                nc.vector.quantize_mx(
+                    out=codes[:, t * P : (t + 1) * P].bitcast(FP8X4),
+                    scales=scales[:, t * P : (t + 1) * P],
+                    in_=grouped[:, t].rearrange("q j c -> q (j c)"),
+                )
             w_codes[w] = codes
             w_scales[w] = scales
 
@@ -120,64 +121,65 @@ def tile_sgan_pa_t_kernel(tc, x, Wq, bq, Wk, bk, fg_sim, out):
 
         def quantise_x(k):
             grouped = x_pool.tile([P, PAIR, N, PACK], BF16, align_bytes=64, name="x_grouped")
-            nc.gpsimd.tensor_scalar(
-                out=grouped[:, 0],
-                in0=x_raw[k][:, 0].rearrange("p t n -> p n t"),
-                scalar1=1.0,
-                scalar2=0.0,
-                op0=MULT,
-                op1=ADD,
-            )
-            regroup(nc.scalar.copy, grouped[:, 1], x_raw[k][:, 1])
-            codes = x_pool.tile([P, COLS], U32, align_bytes=64, name="x_codes")
-            scales = x_pool.tile([P, COLS], U8, align_bytes=64, name="x_scales")
+            for b, image in enumerate(images_of(k)):
+                copy = nc.scalar.copy if b == ROUND_IMAGES[k] - 1 else nc.vector.tensor_copy
+                regroup(copy, grouped[:, b], x_raw[image][:])
+            cols = ROUND_IMAGES[k] * N
+            codes = x_pool.tile([P, PAIR * N], U32, align_bytes=64, name="x_codes")
+            scales = x_pool.tile([P, PAIR * N], U8, align_bytes=64, name="x_scales")
             nc.vector.quantize_mx(
-                out=codes[:].bitcast(FP8X4),
-                scales=scales[:],
-                in_=grouped[:].rearrange("p b n t -> p (b n t)"),
+                out=codes[:, :cols].bitcast(FP8X4),
+                scales=scales[:, :cols],
+                in_=grouped[:, : ROUND_IMAGES[k]].rearrange("p b n t -> p (b n t)"),
             )
             x_mx[k] = (codes, scales)
 
         def project(k):
             codes, scales = x_mx[k]
-            for w in ("q", "k"):
-                plane = work.tile([P, PACK, COLS], BF16, name="planes_" + w)
+            cols = ROUND_IMAGES[k] * N
+            for w in PROJECTIONS:
+                plane = work.tile([P, PACK, PAIR * N], BF16, name="planes_" + w)
                 for t in range(PACK):
-                    bank = banks.tile([P, COLS], F32, tag="bank", name="bank")
+                    bank = banks.tile([P, PAIR * N], F32, tag="bank", name="bank")
                     nc.tensor.matmul_mx(
-                        out=bank[:],
+                        out=bank[:, :cols],
                         lhsT=w_codes[w][:, t * P : (t + 1) * P].bitcast(FP8X4),
                         lhsT_scale=w_scales[w][:, t * P : (t + 1) * P],
-                        rhs=codes[:].bitcast(FP8X4),
-                        rhs_scale=scales[:],
+                        rhs=codes[:, :cols].bitcast(FP8X4),
+                        rhs_scale=scales[:, :cols],
                         start=True,
                         stop=True,
                     )
                     nc.scalar.activation(
-                        out=plane[:, t, :], in_=bank[:], func=IDENTITY, bias=bias[w][:, t : t + 1], scale=1.0
+                        out=plane[:, t, :cols],
+                        in_=bank[:, :cols],
+                        func=IDENTITY,
+                        bias=bias[w][:, t : t + 1],
+                        scale=1.0,
                     )
                 planes[(k, w)] = plane
 
         def requantise(k):
+            cols = ROUND_IMAGES[k] * N
             grouped = {}
-            for w in ("q", "k"):
-                g = work.tile([P, COLS, PACK], BF16, align_bytes=64, name="grouped_" + w)
-                regroup(nc.vector.tensor_copy, g[:], planes[(k, w)][:])
+            for w in PROJECTIONS:
+                g = work.tile([P, PAIR * N, PACK], BF16, align_bytes=64, name="grouped_" + w)
+                regroup(nc.vector.tensor_copy, g[:, :cols, :], planes[(k, w)][:, :, :cols])
                 grouped[w] = g
-            for w in ("q", "k"):
-                codes = work.tile([P, COLS], U32, align_bytes=64, name="codes_" + w)
-                scales = work.tile([P, COLS], U8, align_bytes=64, name="scales_" + w)
+            for w in PROJECTIONS:
+                codes = work.tile([P, PAIR * N], U32, align_bytes=64, name="codes_" + w)
+                scales = work.tile([P, PAIR * N], U8, align_bytes=64, name="scales_" + w)
                 nc.vector.quantize_mx(
-                    out=codes[:].bitcast(FP8X4),
-                    scales=scales[:],
-                    in_=grouped[w][:].rearrange("p n t -> p (n t)"),
+                    out=codes[:, :cols].bitcast(FP8X4),
+                    scales=scales[:, :cols],
+                    in_=grouped[w][:, :cols, :].rearrange("p n t -> p (n t)"),
                 )
                 qk_mx[(k, w)] = (codes, scales)
 
         def similarity(k):
             q_codes, q_scales = qk_mx[(k, "q")]
             k_codes, k_scales = qk_mx[(k, "k")]
-            for b in range(PAIR):
+            for b, image in enumerate(images_of(k)):
                 sim = sims.tile([P, ROW_TILES, N], F32, name="sim")
                 for i in range(ROW_TILES):
                     rows = slice(b * N + i * P, b * N + (i + 1) * P)
@@ -195,13 +197,11 @@ def tile_sgan_pa_t_kernel(tc, x, Wq, bq, Wk, bk, fg_sim, out):
                     out=result[:].rearrange("p i m -> p (i m)"),
                     in0=sim[:].rearrange("p i m -> p (i m)"),
                     scalar=CK**-0.5,
-                    in1=fg[k][:, b].rearrange("p i m -> p (i m)"),
+                    in1=fg[image][:].rearrange("p i m -> p (i m)"),
                     op0=MULT,
                     op1=MULT,
                 )
-                nc.sync.dma_start(
-                    out=out[PAIR * k + b].rearrange("(i p) m -> p i m", p=P), in_=result[:]
-                )
+                nc.sync.dma_start(out=out[image].rearrange("(i p) m -> p i m", p=P), in_=result[:])
 
         for k in range(AHEAD):
             quantise_x(k)

@@ -90,40 +90,52 @@ def tile_sgan_pa_t_kernel(tc, x, Wq, bq, Wk, bk, fg_sim, out):
 
         w_codes = {}
         w_scales = {}
+        w_grouped = {}
+        flipped = {}
         bias = {}
         for w in PROJECTIONS:
-            b_f32 = consts.tile([P, PACK], F32, name="bias_" + w)
-            nc.vector.tensor_copy(out=b_f32[:], in_=bias_bf16[w][:])
-            bias[w] = b_f32
+            w_grouped[w] = consts.tile([P, PACK, P, PACK], BF16, align_bytes=64, name="w_grouped_" + w)
+            w_codes[w] = consts.tile([P, PACK * P], U32, align_bytes=64, name="w_codes_" + w)
+            w_scales[w] = consts.tile([P, PACK * P], U8, align_bytes=64, name="w_scales_" + w)
+            bias[w] = consts.tile([P, PACK], F32, name="bias_" + w)
 
+        def flip_weight(w, t):
             words = w_raw[w][:].bitcast(F32).rearrange("j t (q u) -> j t u q", u=2)
-            grouped = consts.tile([P, PACK, P, PACK], BF16, align_bytes=64, name="w_grouped_" + w)
-            grouped_words = grouped[:].bitcast(F32)
-            codes = consts.tile([P, PACK * P], U32, align_bytes=64, name="w_codes_" + w)
-            scales = consts.tile([P, PACK * P], U8, align_bytes=64, name="w_scales_" + w)
-            for t in range(PACK):
-                flipped = banks.tile([P, 2, P], F32, tag="bank", name="flipped")
-                for u in range(2):
-                    nc.tensor.transpose(flipped[:, u, :], words[:, t, u, :], ident[:])
-                copy = nc.vector.tensor_copy if t % 2 == 0 else nc.scalar.copy
-                copy(out=grouped_words[:, t], in_=flipped[:].rearrange("q u j -> q j u"))
-                nc.vector.quantize_mx(
-                    out=codes[:, t * P : (t + 1) * P].bitcast(FP8X4),
-                    scales=scales[:, t * P : (t + 1) * P],
-                    in_=grouped[:, t].rearrange("q j c -> q (j c)"),
-                )
-            w_codes[w] = codes
-            w_scales[w] = scales
+            bank = banks.tile([P, 2, P], F32, tag="bank", name="flipped")
+            for u in range(2):
+                nc.tensor.transpose(bank[:, u, :], words[:, t, u, :], ident[:])
+            flipped[(w, t)] = bank
+
+        def group_weight(copy, w, t):
+            copy(
+                out=w_grouped[w][:].bitcast(F32)[:, t],
+                in_=flipped[(w, t)][:].rearrange("q u j -> q j u"),
+            )
+
+        def quantise_weight(w, t):
+            nc.vector.quantize_mx(
+                out=w_codes[w][:, t * P : (t + 1) * P].bitcast(FP8X4),
+                scales=w_scales[w][:, t * P : (t + 1) * P],
+                in_=w_grouped[w][:, t].rearrange("q j c -> q (j c)"),
+            )
+
+        def widen_bias(w):
+            nc.vector.tensor_copy(out=bias[w][:], in_=bias_bf16[w][:])
 
         x_mx = {}
         planes = {}
         qk_mx = {}
 
-        def quantise_x(k):
+        x_grouped = {}
+
+        def regroup_x(k, copies):
             grouped = x_pool.tile([P, PAIR, N, PACK], BF16, align_bytes=64, name="x_grouped")
             for b, image in enumerate(images_of(k)):
-                copy = nc.scalar.copy if b == ROUND_IMAGES[k] - 1 else nc.vector.tensor_copy
-                regroup(copy, grouped[:, b], x_raw[image][:])
+                regroup(copies[b], grouped[:, b], x_raw[image][:])
+            x_grouped[k] = grouped
+
+        def quantise_x(k):
+            grouped = x_grouped[k]
             cols = ROUND_IMAGES[k] * N
             codes = x_pool.tile([P, PAIR * N], U32, align_bytes=64, name="x_codes")
             scales = x_pool.tile([P, PAIR * N], U8, align_bytes=64, name="x_scales")
@@ -134,30 +146,29 @@ def tile_sgan_pa_t_kernel(tc, x, Wq, bq, Wk, bk, fg_sim, out):
             )
             x_mx[k] = (codes, scales)
 
-        def project(k):
+        def project(k, w):
             codes, scales = x_mx[k]
             cols = ROUND_IMAGES[k] * N
-            for w in PROJECTIONS:
-                plane = work.tile([P, PACK, PAIR * N], BF16, name="planes_" + w)
-                for t in range(PACK):
-                    bank = banks.tile([P, PAIR * N], F32, tag="bank", name="bank")
-                    nc.tensor.matmul_mx(
-                        out=bank[:, :cols],
-                        lhsT=w_codes[w][:, t * P : (t + 1) * P].bitcast(FP8X4),
-                        lhsT_scale=w_scales[w][:, t * P : (t + 1) * P],
-                        rhs=codes[:, :cols].bitcast(FP8X4),
-                        rhs_scale=scales[:, :cols],
-                        start=True,
-                        stop=True,
-                    )
-                    nc.scalar.activation(
-                        out=plane[:, t, :cols],
-                        in_=bank[:, :cols],
-                        func=IDENTITY,
-                        bias=bias[w][:, t : t + 1],
-                        scale=1.0,
-                    )
-                planes[(k, w)] = plane
+            plane = work.tile([P, PACK, PAIR * N], BF16, name="planes_" + w)
+            for t in range(PACK):
+                bank = banks.tile([P, PAIR * N], F32, tag="bank", name="bank")
+                nc.tensor.matmul_mx(
+                    out=bank[:, :cols],
+                    lhsT=w_codes[w][:, t * P : (t + 1) * P].bitcast(FP8X4),
+                    lhsT_scale=w_scales[w][:, t * P : (t + 1) * P],
+                    rhs=codes[:, :cols].bitcast(FP8X4),
+                    rhs_scale=scales[:, :cols],
+                    start=True,
+                    stop=True,
+                )
+                nc.scalar.activation(
+                    out=plane[:, t, :cols],
+                    in_=bank[:, :cols],
+                    func=IDENTITY,
+                    bias=bias[w][:, t : t + 1],
+                    scale=1.0,
+                )
+            planes[(k, w)] = plane
 
         def requantise(k):
             cols = ROUND_IMAGES[k] * N
@@ -203,13 +214,48 @@ def tile_sgan_pa_t_kernel(tc, x, Wq, bq, Wk, bk, fg_sim, out):
                 )
                 nc.sync.dma_start(out=out[image].rearrange("(i p) m -> p i m", p=P), in_=result[:])
 
-        for k in range(AHEAD):
-            quantise_x(k)
+        scalar_copy = nc.scalar.copy
+        vector_copy = nc.vector.tensor_copy
+        head_engines = {mybir.EngineType.PE, mybir.EngineType.DVE, mybir.EngineType.Activation}
+        with tc.manual_schedule(engines=head_engines):
+            regroup_x(0, [scalar_copy])
+            for t in range(PACK):
+                flip_weight("q", t)
+            group_weight(vector_copy, "q", 0)
+            quantise_x(0)
+            group_weight(scalar_copy, "q", 1)
+            quantise_weight("q", 0)
+            widen_bias("q")
+            group_weight(vector_copy, "q", 2)
+            quantise_weight("q", 1)
+            group_weight(scalar_copy, "q", 3)
+            quantise_weight("q", 2)
+            quantise_weight("q", 3)
+            project(0, "q")
+            regroup_x(1, [vector_copy])
+            for t in range(PACK):
+                flip_weight("k", t)
+            group_weight(vector_copy, "k", 0)
+            quantise_x(1)
+            group_weight(scalar_copy, "k", 1)
+            quantise_weight("k", 0)
+            widen_bias("k")
+            group_weight(vector_copy, "k", 2)
+            quantise_weight("k", 1)
+            group_weight(scalar_copy, "k", 3)
+            quantise_weight("k", 2)
+            quantise_weight("k", 3)
+            project(0, "k")
+            regroup_x(2, [vector_copy, scalar_copy])
+
         for k in range(ROUNDS + 2):
-            if k + AHEAD < ROUNDS:
+            if 0 < k < ROUNDS - AHEAD:
+                regroup_x(k + AHEAD, ([vector_copy] if ROUND_IMAGES[k + AHEAD] == PAIR else []) + [scalar_copy])
+            if k < ROUNDS - AHEAD:
                 quantise_x(k + AHEAD)
-            if k < ROUNDS:
-                project(k)
+            if 0 < k < ROUNDS:
+                for w in PROJECTIONS:
+                    project(k, w)
             if 1 <= k <= ROUNDS:
                 requantise(k - 1)
             if k >= 2:

@@ -19,11 +19,14 @@ P = 128
 PACK = 4
 PAIR = 2
 ROW_TILES = N // P
+LINE = 8
 RUN = 4
 AHEAD = 2
 ROUND_IMAGES = (1, 1) + (2,) * 14 + (1, 1)
 ROUNDS = len(ROUND_IMAGES)
 PROJECTIONS = ("q", "k")
+EARLY_ROUNDS = 6
+LATE_ROUNDS = 3
 
 FLOPS = IMAGES * (2 * 2 * CK * C * N + 2 * N * N * CK)
 
@@ -45,7 +48,8 @@ def tile_sgan_pa_t_kernel(tc, x, Wq, bq, Wk, bk, fg_sim, out):
         x_pool = ctx.enter_context(tc.tile_pool(name="x_pool", bufs=AHEAD + 2))
         work = ctx.enter_context(tc.tile_pool(name="work", bufs=2))
         results = ctx.enter_context(tc.tile_pool(name="results", bufs=12))
-        banks = ctx.enter_context(tc.psum_pool(name="banks", bufs=6))
+        banks = ctx.enter_context(tc.psum_pool(name="banks", bufs=4))
+        x_banks = ctx.enter_context(tc.psum_pool(name="x_banks", bufs=2))
         sims = ctx.enter_context(tc.psum_pool(name="sims", bufs=2))
 
         def images_of(k):
@@ -87,6 +91,8 @@ def tile_sgan_pa_t_kernel(tc, x, Wq, bq, Wk, bk, fg_sim, out):
 
         ident = consts.tile([P, P], F32, name="ident")
         make_identity(nc, ident[:])
+        ident_bf16 = consts.tile([P, P], BF16, name="ident_bf16")
+        make_identity(nc, ident_bf16[:])
 
         w_codes = {}
         w_scales = {}
@@ -128,11 +134,29 @@ def tile_sgan_pa_t_kernel(tc, x, Wq, bq, Wk, bk, fg_sim, out):
 
         x_grouped = {}
 
-        def regroup_x(k, copies):
-            grouped = x_pool.tile([P, PAIR, N, PACK], BF16, align_bytes=64, name="x_grouped")
-            for b, image in enumerate(images_of(k)):
-                regroup(copies[b], grouped[:, b], x_raw[image][:])
-            x_grouped[k] = grouped
+        def regroup_x(k, b, copy):
+            if b == 0:
+                x_grouped[k] = x_pool.tile([P, PAIR, N, PACK], BF16, align_bytes=64, name="x_grouped")
+            regroup(copy, x_grouped[k][:, b], x_raw[images_of(k)[b]][:])
+
+        def regroup_x_by_product(k, b):
+            if b == 0:
+                x_grouped[k] = x_pool.tile([P, PAIR, N, PACK], BF16, align_bytes=64, name="x_grouped")
+            raw = x_raw[images_of(k)[b]]
+            bank = x_banks.tile([P, N, PACK], BF16, name="x_bank")
+            for h in range(2):
+                half = slice(h * P, (h + 1) * P)
+                nc.tensor.matmul(
+                    out=bank[:, half, :].rearrange("p (c i) t -> p c t i", i=LINE),
+                    lhsT=ident_bf16[:],
+                    rhs=raw[:, :, half].rearrange("p t (c i) -> p c t i", i=LINE),
+                    start=True,
+                    stop=True,
+                )
+            nc.scalar.copy(
+                out=x_grouped[k][:, b].rearrange("p n t -> p (n t)"),
+                in_=bank[:].rearrange("p n t -> p (n t)"),
+            )
 
         def quantise_x(k):
             grouped = x_grouped[k]
@@ -170,22 +194,29 @@ def tile_sgan_pa_t_kernel(tc, x, Wq, bq, Wk, bk, fg_sim, out):
                 )
             planes[(k, w)] = plane
 
-        def requantise(k):
+        qk_grouped = {}
+
+        def regroup_qk(k, w):
             cols = ROUND_IMAGES[k] * N
-            grouped = {}
-            for w in PROJECTIONS:
-                g = work.tile([P, PAIR * N, PACK], BF16, align_bytes=64, name="grouped_" + w)
-                regroup(nc.vector.tensor_copy, g[:, :cols, :], planes[(k, w)][:, :, :cols])
-                grouped[w] = g
-            for w in PROJECTIONS:
-                codes = work.tile([P, PAIR * N], U32, align_bytes=64, name="codes_" + w)
-                scales = work.tile([P, PAIR * N], U8, align_bytes=64, name="scales_" + w)
-                nc.vector.quantize_mx(
-                    out=codes[:, :cols].bitcast(FP8X4),
-                    scales=scales[:, :cols],
-                    in_=grouped[w][:, :cols, :].rearrange("p n t -> p (n t)"),
-                )
-                qk_mx[(k, w)] = (codes, scales)
+            grouped = work.tile([P, PAIR * N, PACK], BF16, align_bytes=64, name="grouped_" + w)
+            cut = cols // 2 if w == "k" and k >= ROUNDS - LATE_ROUNDS else cols
+            regroup(nc.vector.tensor_copy, grouped[:, :cut, :], planes[(k, w)][:, :, :cut])
+            if cut < cols:
+                regroup(nc.scalar.copy, grouped[:, cut:cols, :], planes[(k, w)][:, :, cut:cols])
+            qk_grouped[(k, w)] = grouped
+
+        def quantise_qk(k, w):
+            cols = ROUND_IMAGES[k] * N
+            codes = work.tile([P, PAIR * N], U32, align_bytes=64, name="codes_" + w)
+            scales = work.tile([P, PAIR * N], U8, align_bytes=64, name="scales_" + w)
+            nc.vector.quantize_mx(
+                out=codes[:, :cols].bitcast(FP8X4),
+                scales=scales[:, :cols],
+                in_=qk_grouped[(k, w)][:, :cols, :].rearrange("p n t -> p (n t)"),
+            )
+            qk_mx[(k, w)] = (codes, scales)
+
+        sim_banks = {}
 
         def similarity(k):
             q_codes, q_scales = qk_mx[(k, "q")]
@@ -203,10 +234,14 @@ def tile_sgan_pa_t_kernel(tc, x, Wq, bq, Wk, bk, fg_sim, out):
                         start=True,
                         stop=True,
                     )
+                sim_banks[image] = sim
+
+        def finish(k):
+            for image in images_of(k):
                 result = results.tile([P, ROW_TILES, N], F32, name="result")
                 nc.vector.scalar_tensor_tensor(
                     out=result[:].rearrange("p i m -> p (i m)"),
-                    in0=sim[:].rearrange("p i m -> p (i m)"),
+                    in0=sim_banks[image][:].rearrange("p i m -> p (i m)"),
                     scalar=CK**-0.5,
                     in1=fg[image][:].rearrange("p i m -> p (i m)"),
                     op0=MULT,
@@ -218,7 +253,7 @@ def tile_sgan_pa_t_kernel(tc, x, Wq, bq, Wk, bk, fg_sim, out):
         vector_copy = nc.vector.tensor_copy
         head_engines = {mybir.EngineType.PE, mybir.EngineType.DVE, mybir.EngineType.Activation}
         with tc.manual_schedule(engines=head_engines):
-            regroup_x(0, [scalar_copy])
+            regroup_x(0, 0, scalar_copy)
             for t in range(PACK):
                 flip_weight("q", t)
             group_weight(vector_copy, "q", 0)
@@ -232,7 +267,7 @@ def tile_sgan_pa_t_kernel(tc, x, Wq, bq, Wk, bk, fg_sim, out):
             quantise_weight("q", 2)
             quantise_weight("q", 3)
             project(0, "q")
-            regroup_x(1, [vector_copy])
+            regroup_x(1, 0, vector_copy)
             for t in range(PACK):
                 flip_weight("k", t)
             group_weight(vector_copy, "k", 0)
@@ -246,17 +281,32 @@ def tile_sgan_pa_t_kernel(tc, x, Wq, bq, Wk, bk, fg_sim, out):
             quantise_weight("k", 2)
             quantise_weight("k", 3)
             project(0, "k")
-            regroup_x(2, [vector_copy, scalar_copy])
+            regroup_x(2, 0, vector_copy)
+            regroup_x(2, 1, vector_copy)
 
-        for k in range(ROUNDS + 2):
-            if 0 < k < ROUNDS - AHEAD:
-                regroup_x(k + AHEAD, ([vector_copy] if ROUND_IMAGES[k + AHEAD] == PAIR else []) + [scalar_copy])
-            if k < ROUNDS - AHEAD:
-                quantise_x(k + AHEAD)
-            if 0 < k < ROUNDS:
-                for w in PROJECTIONS:
-                    project(k, w)
-            if 1 <= k <= ROUNDS:
-                requantise(k - 1)
-            if k >= 2:
-                similarity(k - 2)
+            for k in range(ROUNDS + 2):
+                if 0 < k < ROUNDS:
+                    project(k, "q")
+                if k >= 2:
+                    similarity(k - 2)
+                if 1 <= k <= ROUNDS:
+                    regroup_qk(k - 1, "q")
+                ahead = k + AHEAD + 1
+                if ahead < EARLY_ROUNDS:
+                    for b in range(PAIR):
+                        regroup_x(ahead, b, vector_copy)
+                elif ahead < ROUNDS:
+                    regroup_x_by_product(ahead, 0)
+                if 1 <= k <= ROUNDS:
+                    regroup_qk(k - 1, "k")
+                    quantise_qk(k - 1, "q")
+                if 0 < k < ROUNDS:
+                    project(k, "k")
+                if EARLY_ROUNDS <= ahead < ROUNDS and ROUND_IMAGES[ahead] == PAIR:
+                    regroup_x_by_product(ahead, 1)
+                if k + AHEAD < ROUNDS:
+                    quantise_x(k + AHEAD)
+                if 1 <= k <= ROUNDS:
+                    quantise_qk(k - 1, "k")
+                if k >= 2:
+                    finish(k - 2)

@@ -25,8 +25,11 @@ AHEAD = 2
 ROUND_IMAGES = (1, 1) + (2,) * 14 + (1, 1)
 ROUNDS = len(ROUND_IMAGES)
 PROJECTIONS = ("q", "k")
-EARLY_ROUNDS = 6
-LATE_ROUNDS = 3
+EARLY_ROUNDS = 4
+VECTOR_EVERY = 3
+LATE_ROUNDS = 2
+SCALAR_QUARTERS = {"q": 1, "k": 3}
+LEAD_IMAGES = 6
 
 FLOPS = IMAGES * (2 * 2 * CK * C * N + 2 * N * N * CK)
 
@@ -59,7 +62,7 @@ def tile_sgan_pa_t_kernel(tc, x, Wq, bq, Wk, bk, fg_sim, out):
         x_raw = {}
         fg = {}
         w_raw = {}
-        bias_bf16 = {}
+        bias = {}
 
         def load_x(image):
             raw = inputs.tile([P, PACK, N], BF16, name="x_raw")
@@ -71,23 +74,29 @@ def tile_sgan_pa_t_kernel(tc, x, Wq, bq, Wk, bk, fg_sim, out):
             nc.sync.dma_start(out=mask[:], in_=fg_sim[image].rearrange("(i p) m -> p i m", p=P))
             fg[image] = mask
 
-        def load_weight(w, weight, b_vec):
-            raw = consts.tile([P, PACK, C], BF16, name="w_raw_" + w)
-            nc.sync.dma_start(out=raw[:], in_=weight.rearrange("(p t) c -> p t c", t=PACK))
-            w_raw[w] = raw
-            b_raw = consts.tile([P, PACK], BF16, name="bias_bf16_" + w)
-            nc.scalar.dma_start(out=b_raw[:], in_=b_vec.rearrange("(p t) -> p t", t=PACK))
-            bias_bf16[w] = b_raw
+        def load_weight(w, weight, t):
+            raw = consts.tile([P, C], BF16, name=f"w_raw_{w}{t}")
+            nc.sync.dma_start(out=raw[:], in_=weight.rearrange("(p t) c -> p t c", t=PACK)[:, t])
+            w_raw[(w, t)] = raw
 
+        def load_bias(w, b_vec):
+            bias[w] = consts.tile([P, PACK], BF16, name="bias_" + w)
+            nc.scalar.dma_start(out=bias[w][:], in_=b_vec.rearrange("(p t) -> p t", t=PACK))
+
+        load_bias("q", bq)
+        load_bias("k", bk)
+        load_weight("q", Wq, 0)
         load_x(0)
-        load_weight("q", Wq, bq)
-        load_x(1)
-        load_weight("k", Wk, bk)
-        for image in range(2, IMAGES):
+        for t in range(1, PACK):
+            load_weight("q", Wq, t)
+        for t in range(PACK):
+            load_weight("k", Wk, t)
+        for image in range(1, LEAD_IMAGES + 1):
             load_x(image)
-            load_fg(image - 2)
-        load_fg(IMAGES - 2)
-        load_fg(IMAGES - 1)
+        for image in range(IMAGES):
+            load_fg(image)
+            if image + LEAD_IMAGES + 1 < IMAGES:
+                load_x(image + LEAD_IMAGES + 1)
 
         ident = consts.tile([P, P], F32, name="ident")
         make_identity(nc, ident[:])
@@ -98,18 +107,16 @@ def tile_sgan_pa_t_kernel(tc, x, Wq, bq, Wk, bk, fg_sim, out):
         w_scales = {}
         w_grouped = {}
         flipped = {}
-        bias = {}
         for w in PROJECTIONS:
             w_grouped[w] = consts.tile([P, PACK, P, PACK], BF16, align_bytes=64, name="w_grouped_" + w)
             w_codes[w] = consts.tile([P, PACK * P], U32, align_bytes=64, name="w_codes_" + w)
             w_scales[w] = consts.tile([P, PACK * P], U8, align_bytes=64, name="w_scales_" + w)
-            bias[w] = consts.tile([P, PACK], F32, name="bias_" + w)
 
         def flip_weight(w, t):
-            words = w_raw[w][:].bitcast(F32).rearrange("j t (q u) -> j t u q", u=2)
+            words = w_raw[(w, t)][:].bitcast(F32).rearrange("j (q u) -> j u q", u=2)
             bank = banks.tile([P, 2, P], F32, tag="bank", name="flipped")
             for u in range(2):
-                nc.tensor.transpose(bank[:, u, :], words[:, t, u, :], ident[:])
+                nc.tensor.transpose(bank[:, u, :], words[:, u, :], ident[:])
             flipped[(w, t)] = bank
 
         def group_weight(copy, w, t):
@@ -124,9 +131,6 @@ def tile_sgan_pa_t_kernel(tc, x, Wq, bq, Wk, bk, fg_sim, out):
                 scales=w_scales[w][:, t * P : (t + 1) * P],
                 in_=w_grouped[w][:, t].rearrange("q j c -> q (j c)"),
             )
-
-        def widen_bias(w):
-            nc.vector.tensor_copy(out=bias[w][:], in_=bias_bf16[w][:])
 
         x_mx = {}
         planes = {}
@@ -199,7 +203,7 @@ def tile_sgan_pa_t_kernel(tc, x, Wq, bq, Wk, bk, fg_sim, out):
         def regroup_qk(k, w):
             cols = ROUND_IMAGES[k] * N
             grouped = work.tile([P, PAIR * N, PACK], BF16, align_bytes=64, name="grouped_" + w)
-            cut = cols // 2 if w == "k" and k >= ROUNDS - LATE_ROUNDS else cols
+            cut = cols - cols // 4 * SCALAR_QUARTERS[w] if k >= ROUNDS - LATE_ROUNDS else cols
             regroup(nc.vector.tensor_copy, grouped[:, :cut, :], planes[(k, w)][:, :, :cut])
             if cut < cols:
                 regroup(nc.scalar.copy, grouped[:, cut:cols, :], planes[(k, w)][:, :, cut:cols])
@@ -253,35 +257,31 @@ def tile_sgan_pa_t_kernel(tc, x, Wq, bq, Wk, bk, fg_sim, out):
         vector_copy = nc.vector.tensor_copy
         head_engines = {mybir.EngineType.PE, mybir.EngineType.DVE, mybir.EngineType.Activation}
         with tc.manual_schedule(engines=head_engines):
-            regroup_x(0, 0, scalar_copy)
-            for t in range(PACK):
+            flip_weight("q", 0)
+            group_weight(scalar_copy, "q", 0)
+            regroup_x(0, 0, vector_copy)
+            for t in range(1, PACK):
                 flip_weight("q", t)
-            group_weight(vector_copy, "q", 0)
-            quantise_x(0)
-            group_weight(scalar_copy, "q", 1)
+                group_weight(scalar_copy, "q", t)
             quantise_weight("q", 0)
-            widen_bias("q")
-            group_weight(vector_copy, "q", 2)
-            quantise_weight("q", 1)
-            group_weight(scalar_copy, "q", 3)
-            quantise_weight("q", 2)
-            quantise_weight("q", 3)
+            quantise_x(0)
+            for t in range(1, PACK):
+                quantise_weight("q", t)
             project(0, "q")
-            regroup_x(1, 0, vector_copy)
             for t in range(PACK):
                 flip_weight("k", t)
             group_weight(vector_copy, "k", 0)
-            quantise_x(1)
-            group_weight(scalar_copy, "k", 1)
+            group_weight(vector_copy, "k", 1)
             quantise_weight("k", 0)
-            widen_bias("k")
-            group_weight(vector_copy, "k", 2)
+            group_weight(scalar_copy, "k", 2)
             quantise_weight("k", 1)
+            regroup_x(1, 0, vector_copy)
             group_weight(scalar_copy, "k", 3)
             quantise_weight("k", 2)
             quantise_weight("k", 3)
             project(0, "k")
             regroup_x(2, 0, vector_copy)
+            quantise_x(1)
             regroup_x(2, 1, vector_copy)
 
             for k in range(ROUNDS + 2):
@@ -292,17 +292,21 @@ def tile_sgan_pa_t_kernel(tc, x, Wq, bq, Wk, bk, fg_sim, out):
                 if 1 <= k <= ROUNDS:
                     regroup_qk(k - 1, "q")
                 ahead = k + AHEAD + 1
-                if ahead < EARLY_ROUNDS:
-                    for b in range(PAIR):
-                        regroup_x(ahead, b, vector_copy)
-                elif ahead < ROUNDS:
+                by_product = range(EARLY_ROUNDS, ROUNDS)
+                second = ahead < ROUNDS and ROUND_IMAGES[ahead] == PAIR
+                second_by_product = second and ahead in by_product and ahead % VECTOR_EVERY > 0
+                if ahead in by_product:
                     regroup_x_by_product(ahead, 0)
+                elif ahead < ROUNDS:
+                    regroup_x(ahead, 0, vector_copy)
+                if second and not second_by_product:
+                    regroup_x(ahead, 1, vector_copy)
                 if 1 <= k <= ROUNDS:
                     regroup_qk(k - 1, "k")
                     quantise_qk(k - 1, "q")
                 if 0 < k < ROUNDS:
                     project(k, "k")
-                if EARLY_ROUNDS <= ahead < ROUNDS and ROUND_IMAGES[ahead] == PAIR:
+                if second_by_product:
                     regroup_x_by_product(ahead, 1)
                 if k + AHEAD < ROUNDS:
                     quantise_x(k + AHEAD)

@@ -26,9 +26,8 @@ ROUND_IMAGES = (1, 1) + (2,) * 14 + (1, 1)
 ROUNDS = len(ROUND_IMAGES)
 PROJECTIONS = ("q", "k")
 EARLY_ROUNDS = 4
-VECTOR_EVERY = 3
-LATE_ROUNDS = 2
-SCALAR_QUARTERS = {"q": 1, "k": 3}
+VECTOR_EVERY = 5
+SHARED_ROUNDS = {"q": 1, "k": 3}
 LEAD_IMAGES = 6
 
 FLOPS = IMAGES * (2 * 2 * CK * C * N + 2 * N * N * CK)
@@ -203,7 +202,7 @@ def tile_sgan_pa_t_kernel(tc, x, Wq, bq, Wk, bk, fg_sim, out):
         def regroup_qk(k, w):
             cols = ROUND_IMAGES[k] * N
             grouped = work.tile([P, PAIR * N, PACK], BF16, align_bytes=64, name="grouped_" + w)
-            cut = cols - cols // 4 * SCALAR_QUARTERS[w] if k >= ROUNDS - LATE_ROUNDS else cols
+            cut = cols // 2 if k >= ROUNDS - SHARED_ROUNDS[w] else cols
             regroup(nc.vector.tensor_copy, grouped[:, :cut, :], planes[(k, w)][:, :, :cut])
             if cut < cols:
                 regroup(nc.scalar.copy, grouped[:, cut:cols, :], planes[(k, w)][:, :, cut:cols])
@@ -243,15 +242,19 @@ def tile_sgan_pa_t_kernel(tc, x, Wq, bq, Wk, bk, fg_sim, out):
         def finish(k):
             for image in images_of(k):
                 result = results.tile([P, ROW_TILES, N], F32, name="result")
-                nc.vector.scalar_tensor_tensor(
-                    out=result[:].rearrange("p i m -> p (i m)"),
-                    in0=sim_banks[image][:].rearrange("p i m -> p (i m)"),
-                    scalar=CK**-0.5,
-                    in1=fg[image][:].rearrange("p i m -> p (i m)"),
-                    op0=MULT,
-                    op1=MULT,
-                )
-                nc.sync.dma_start(out=out[image].rearrange("(i p) m -> p i m", p=P), in_=result[:])
+                store = out[image].rearrange("(i p) m -> p i m", p=P)
+                pieces = ROW_TILES if image == IMAGES - 1 else 1
+                for piece in range(pieces):
+                    rows = slice(piece * ROW_TILES // pieces, (piece + 1) * ROW_TILES // pieces)
+                    nc.vector.scalar_tensor_tensor(
+                        out=result[:, rows].rearrange("p i m -> p (i m)"),
+                        in0=sim_banks[image][:, rows].rearrange("p i m -> p (i m)"),
+                        scalar=CK**-0.5,
+                        in1=fg[image][:, rows].rearrange("p i m -> p (i m)"),
+                        op0=MULT,
+                        op1=MULT,
+                    )
+                    nc.sync.dma_start(out=store[:, rows], in_=result[:, rows])
 
         scalar_copy = nc.scalar.copy
         vector_copy = nc.vector.tensor_copy

from contextlib import ExitStack

import concourse.mybir as mybir
from concourse.masks import make_identity

F32 = mybir.dt.float32
BF16 = mybir.dt.bfloat16
U32 = mybir.dt.uint32
U8 = mybir.dt.uint8
FP8X4 = mybir.dt.float8_e4m3fn_x4
IDENTITY = mybir.ActivationFunctionType.Identity
MULT = mybir.AluOpType.mult

IMAGES = 32
C = 512
CK = 512
N = 256
P = 128
PACK = 4
PAIR = 2
ROW_TILES = N // P
LINE = 8
RUN = 4
AHEAD = 2
ROUND_IMAGES = (1, 1) + (2,) * 14 + (1, 1)
ROUNDS = len(ROUND_IMAGES)
PROJECTIONS = ("q", "k")
EARLY_ROUNDS = 4
VECTOR_EVERY = 5
SHARED_ROUNDS = {"q": 1, "k": 3}
LEAD_IMAGES = 6

FLOPS = IMAGES * (2 * 2 * CK * C * N + 2 * N * N * CK)

assert sum(ROUND_IMAGES) == IMAGES


def regroup(copy, grouped, planes):
    copy(
        out=grouped.rearrange("p (c i) t -> p c t i", i=RUN),
        in_=planes.rearrange("p t (c i) -> p c t i", i=RUN),
    )


def tile_sgan_pa_t_kernel(tc, x, Wq, bq, Wk, bk, fg_sim, out):
    nc = tc.nc
    with ExitStack() as ctx:
        consts = ctx.enter_context(tc.tile_pool(name="consts", bufs=1))
        inputs = ctx.enter_context(tc.tile_pool(name="inputs", bufs=IMAGES))
        x_pool = ctx.enter_context(tc.tile_pool(name="x_pool", bufs=AHEAD + 2))
        work = ctx.enter_context(tc.tile_pool(name="work", bufs=2))
        results = ctx.enter_context(tc.tile_pool(name="results", bufs=12))
        banks = ctx.enter_context(tc.psum_pool(name="banks", bufs=4))
        x_banks = ctx.enter_context(tc.psum_pool(name="x_banks", bufs=2))
        sims = ctx.enter_context(tc.psum_pool(name="sims", bufs=2))

        def images_of(k):
            first = sum(ROUND_IMAGES[:k])
            return range(first, first + ROUND_IMAGES[k])

        x_raw = {}
        fg = {}
        w_raw = {}
        bias = {}

        def load_x(image):
            raw = inputs.tile([P, PACK, N], BF16, name="x_raw")
            nc.sync.dma_start(out=raw[:], in_=x[image].rearrange("(p t) h w -> p t (h w)", t=PACK))
            x_raw[image] = raw

        def load_fg(image):
            mask = inputs.tile([P, ROW_TILES, N], BF16, name="fg")
            nc.sync.dma_start(out=mask[:], in_=fg_sim[image].rearrange("(i p) m -> p i m", p=P))
            fg[image] = mask

        def load_weight(w, weight, t):
            raw = consts.tile([P, C], BF16, name=f"w_raw_{w}{t}")
            nc.sync.dma_start(out=raw[:], in_=weight.rearrange("(p t) c -> p t c", t=PACK)[:, t])
            w_raw[(w, t)] = raw

        def load_bias(w, b_vec):
            bias[w] = consts.tile([P, PACK], BF16, name="bias_" + w)
            nc.scalar.dma_start(out=bias[w][:], in_=b_vec.rearrange("(p t) -> p t", t=PACK))

        load_bias("q", bq)
        load_bias("k", bk)
        load_weight("q", Wq, 0)
        load_x(0)
        for t in range(1, PACK):
            load_weight("q", Wq, t)
        for t in range(PACK):
            load_weight("k", Wk, t)
        for image in range(1, LEAD_IMAGES + 1):
            load_x(image)
        for image in range(IMAGES):
            load_fg(image)
            if image + LEAD_IMAGES + 1 < IMAGES:
                load_x(image + LEAD_IMAGES + 1)

        ident = consts.tile([P, P], F32, name="ident")
        make_identity(nc, ident[:])
        ident_bf16 = consts.tile([P, P], BF16, name="ident_bf16")
        make_identity(nc, ident_bf16[:])

        w_codes = {}
        w_scales = {}
        w_grouped = {}
        flipped = {}
        for w in PROJECTIONS:
            w_grouped[w] = consts.tile([P, PACK, P, PACK], BF16, align_bytes=64, name="w_grouped_" + w)
            w_codes[w] = consts.tile([P, PACK * P], U32, align_bytes=64, name="w_codes_" + w)
            w_scales[w] = consts.tile([P, PACK * P], U8, align_bytes=64, name="w_scales_" + w)

        def flip_weight(w, t):
            words = w_raw[(w, t)][:].bitcast(F32).rearrange("j (q u) -> j u q", u=2)
            bank = banks.tile([P, 2, P], F32, tag="bank", name="flipped")
            for u in range(2):
                nc.tensor.transpose(bank[:, u, :], words[:, u, :], ident[:])
            flipped[(w, t)] = bank

        def group_weight(copy, w, t):
            copy(
                out=w_grouped[w][:].bitcast(F32)[:, t],
                in_=flipped[(w, t)][:].rearrange("q u j -> q j u"),
            )

        def quantise_weight(w, t):
            nc.vector.quantize_mx(
                out=w_codes[w][:, t * P : (t + 1) * P].bitcast(FP8X4),
                scales=w_scales[w][:, t * P : (t + 1) * P],
                in_=w_grouped[w][:, t].rearrange("q j c -> q (j c)"),
            )

        x_mx = {}
        planes = {}
        qk_mx = {}

        x_grouped = {}

        def regroup_x(k, b, copy):
            if b == 0:
                x_grouped[k] = x_pool.tile([P, PAIR, N, PACK], BF16, align_bytes=64, name="x_grouped")
            regroup(copy, x_grouped[k][:, b], x_raw[images_of(k)[b]][:])

        def regroup_x_by_product(k, b):
            if b == 0:
                x_grouped[k] = x_pool.tile([P, PAIR, N, PACK], BF16, align_bytes=64, name="x_grouped")
            raw = x_raw[images_of(k)[b]]
            bank = x_banks.tile([P, N, PACK], BF16, name="x_bank")
            for h in range(2):
                half = slice(h * P, (h + 1) * P)
                nc.tensor.matmul(
                    out=bank[:, half, :].rearrange("p (c i) t -> p c t i", i=LINE),
                    lhsT=ident_bf16[:],
                    rhs=raw[:, :, half].rearrange("p t (c i) -> p c t i", i=LINE),
                    start=True,
                    stop=True,
                )
            nc.scalar.copy(
                out=x_grouped[k][:, b].rearrange("p n t -> p (n t)"),
                in_=bank[:].rearrange("p n t -> p (n t)"),
            )

        def quantise_x(k):
            grouped = x_grouped[k]
            cols = ROUND_IMAGES[k] * N
            codes = x_pool.tile([P, PAIR * N], U32, align_bytes=64, name="x_codes")
            scales = x_pool.tile([P, PAIR * N], U8, align_bytes=64, name="x_scales")
            nc.vector.quantize_mx(
                out=codes[:, :cols].bitcast(FP8X4),
                scales=scales[:, :cols],
                in_=grouped[:, : ROUND_IMAGES[k]].rearrange("p b n t -> p (b n t)"),
            )
            x_mx[k] = (codes, scales)

        def project(k, w):
            codes, scales = x_mx[k]
            cols = ROUND_IMAGES[k] * N
            plane = work.tile([P, PACK, PAIR * N], BF16, name="planes_" + w)
            for t in range(PACK):
                bank = banks.tile([P, PAIR * N], F32, tag="bank", name="bank")
                nc.tensor.matmul_mx(
                    out=bank[:, :cols],
                    lhsT=w_codes[w][:, t * P : (t + 1) * P].bitcast(FP8X4),
                    lhsT_scale=w_scales[w][:, t * P : (t + 1) * P],
                    rhs=codes[:, :cols].bitcast(FP8X4),
                    rhs_scale=scales[:, :cols],
                    start=True,
                    stop=True,
                )
                nc.scalar.activation(
                    out=plane[:, t, :cols],
                    in_=bank[:, :cols],
                    func=IDENTITY,
                    bias=bias[w][:, t : t + 1],
                    scale=1.0,
                )
            planes[(k, w)] = plane

        qk_grouped = {}

        def regroup_qk(k, w):
            cols = ROUND_IMAGES[k] * N
            grouped = work.tile([P, PAIR * N, PACK], BF16, align_bytes=64, name="grouped_" + w)
            cut = cols // 2 if k >= ROUNDS - SHARED_ROUNDS[w] else cols
            regroup(nc.vector.tensor_copy, grouped[:, :cut, :], planes[(k, w)][:, :, :cut])
            if cut < cols:
                regroup(nc.scalar.copy, grouped[:, cut:cols, :], planes[(k, w)][:, :, cut:cols])
            qk_grouped[(k, w)] = grouped

        def quantise_qk(k, w):
            cols = ROUND_IMAGES[k] * N
            codes = work.tile([P, PAIR * N], U32, align_bytes=64, name="codes_" + w)
            scales = work.tile([P, PAIR * N], U8, align_bytes=64, name="scales_" + w)
            nc.vector.quantize_mx(
                out=codes[:, :cols].bitcast(FP8X4),
                scales=scales[:, :cols],
                in_=qk_grouped[(k, w)][:, :cols, :].rearrange("p n t -> p (n t)"),
            )
            qk_mx[(k, w)] = (codes, scales)

        sim_banks = {}

        def similarity(k):
            q_codes, q_scales = qk_mx[(k, "q")]
            k_codes, k_scales = qk_mx[(k, "k")]
            for b, image in enumerate(images_of(k)):
                sim = sims.tile([P, ROW_TILES, N], F32, name="sim")
                for i in range(ROW_TILES):
                    rows = slice(b * N + i * P, b * N + (i + 1) * P)
                    nc.tensor.matmul_mx(
                        out=sim[:, i, :],
                        lhsT=q_codes[:, rows].bitcast(FP8X4),
                        lhsT_scale=q_scales[:, rows],
                        rhs=k_codes[:, b * N : (b + 1) * N].bitcast(FP8X4),
                        rhs_scale=k_scales[:, b * N : (b + 1) * N],
                        start=True,
                        stop=True,
                    )
                sim_banks[image] = sim

        def finish(k):
            for image in images_of(k):
                result = results.tile([P, ROW_TILES, N], F32, name="result")
                store = out[image].rearrange("(i p) m -> p i m", p=P)
                pieces = ROW_TILES if image == IMAGES - 1 else 1
                for piece in range(pieces):
                    rows = slice(piece * ROW_TILES // pieces, (piece + 1) * ROW_TILES // pieces)
                    nc.vector.scalar_tensor_tensor(
                        out=result[:, rows].rearrange("p i m -> p (i m)"),
                        in0=sim_banks[image][:, rows].rearrange("p i m -> p (i m)"),
                        scalar=CK**-0.5,
                        in1=fg[image][:, rows].rearrange("p i m -> p (i m)"),
                        op0=MULT,
                        op1=MULT,
                    )
                    nc.sync.dma_start(out=store[:, rows], in_=result[:, rows])

        scalar_copy = nc.scalar.copy
        vector_copy = nc.vector.tensor_copy
        head_engines = {mybir.EngineType.PE, mybir.EngineType.DVE, mybir.EngineType.Activation}
        with tc.manual_schedule(engines=head_engines):
            flip_weight("q", 0)
            group_weight(scalar_copy, "q", 0)
            regroup_x(0, 0, vector_copy)
            for t in range(1, PACK):
                flip_weight("q", t)
                group_weight(scalar_copy, "q", t)
            quantise_weight("q", 0)
            quantise_x(0)
            for t in range(1, PACK):
                quantise_weight("q", t)
            project(0, "q")
            for t in range(PACK):
                flip_weight("k", t)
            group_weight(vector_copy, "k", 0)
            group_weight(vector_copy, "k", 1)
            quantise_weight("k", 0)
            group_weight(scalar_copy, "k", 2)
            quantise_weight("k", 1)
            regroup_x(1, 0, vector_copy)
            group_weight(scalar_copy, "k", 3)
            quantise_weight("k", 2)
            quantise_weight("k", 3)
            project(0, "k")
            regroup_x(2, 0, vector_copy)
            quantise_x(1)
            regroup_x(2, 1, vector_copy)

            for k in range(ROUNDS + 2):
                if 0 < k < ROUNDS:
                    project(k, "q")
                if k >= 2:
                    similarity(k - 2)
                if 1 <= k <= ROUNDS:
                    regroup_qk(k - 1, "q")
                ahead = k + AHEAD + 1
                by_product = range(EARLY_ROUNDS, ROUNDS)
                second = ahead < ROUNDS and ROUND_IMAGES[ahead] == PAIR
                second_by_product = second and ahead in by_product and ahead % VECTOR_EVERY > 0
                if ahead in by_product:
                    regroup_x_by_product(ahead, 0)
                elif ahead < ROUNDS:
                    regroup_x(ahead, 0, vector_copy)
                if second and not second_by_product:
                    regroup_x(ahead, 1, vector_copy)
                if 1 <= k <= ROUNDS:
                    regroup_qk(k - 1, "k")
                    quantise_qk(k - 1, "q")
                if 0 < k < ROUNDS:
                    project(k, "k")
                if second_by_product:
                    regroup_x_by_product(ahead, 1)
                if k + AHEAD < ROUNDS:
                    quantise_x(k + AHEAD)
                if 1 <= k <= ROUNDS:
                    quantise_qk(k - 1, "k")
                if k >= 2:
                    finish(k - 2)
